import numpy as np
import ml_dtypes


def mxq(x, axis, fmt="e4m3"):
    dtype, down = {"e4m3": (ml_dtypes.float8_e4m3fn, 7), "e5m2": (ml_dtypes.float8_e5m2, 14)}[fmt]
    v = np.moveaxis(np.asarray(x, np.float32).astype(ml_dtypes.bfloat16).astype(np.float64), axis, -1)
    blocks = v.reshape(v.shape[:-1] + (-1, 32))
    amax = np.abs(blocks).max(-1, keepdims=True)
    byte = np.maximum(np.where(amax > 0, np.frexp(amax)[1] - 1 + 127, 0) - down, 1)
    scale = np.exp2(byte - 127.0)
    codes = (blocks / scale).astype(np.float32).astype(dtype).astype(np.float64)
    return np.moveaxis((codes * scale).reshape(v.shape), -1, axis)


WIDE = False


def mx_kscale(k):
    if not WIDE:
        return np.ones(k)
    levels = np.array([10, -10, 5, -5, 0])
    a = np.random.permutation(np.resize(levels, k // 512 * 4)).reshape(k // 512, 4)
    idx = np.arange(k)
    return np.exp2(a[idx // 512, idx % 128 // 32])


BF16 = ml_dtypes.bfloat16


def bf(x):
    return np.asarray(x, np.float32).astype(BF16)


def f64(x):
    return np.asarray(x).astype(np.float64)


NM, B, IN, H1, H2, OUT = 8, 512, 512, 1024, 512, 128
LS_LO, LS_HI = -20.0, 4.0


def fnoise(ei, ej):
    return np.sign(ei) * np.sign(ej) * np.sqrt(np.abs(ei)) * np.sqrt(np.abs(ej))


def plin(xq, w, b):
    y = xq.transpose(1, 0, 2) @ mxq(f64(w), 2, 'e4m3').transpose(0, 2, 1)
    return y.transpose(1, 0, 2) + f64(b)[None]


def setup_inputs():
    k = mx_kscale(IN)
    return {'s': bf(np.random.standard_normal((B, NM, IN)) * k),
            'ei1': bf(np.random.standard_normal((B, NM, 1))),
            'ej1': bf(np.random.standard_normal((1, NM, H1))),
            'w11': bf(np.random.standard_normal((NM, H1, IN)) / np.sqrt(IN) / k),
            'b11': bf(np.random.standard_normal((NM, H1)) * 0.3),
            'w12': bf(np.random.standard_normal((NM, H1, IN)) * 1.2 / np.sqrt(IN) / k),
            'b12': bf(np.random.standard_normal((NM, H1)) * 0.3)}


def reference(s, ei1, ej1, w11, b11, w12, b12):
    sq = mxq(f64(s), 2, 'e4m3')
    mu = plin(sq, w11, b11)
    log_sigma = np.clip(plin(sq, w12, b12), LS_LO, LS_HI)
    return np.maximum(mu + fnoise(f64(ei1), f64(ej1)) * np.exp(log_sigma), 0.0)

@@ -1,0 +1,354 @@
+import math
+from contextlib import ExitStack
+
+import concourse.mybir as mybir
+from concourse.masks import make_identity
+
+F32 = mybir.dt.float32
+BF16 = mybir.dt.bfloat16
+U32 = mybir.dt.uint32
+U8 = mybir.dt.uint8
+FP8X4 = mybir.dt.float8_e4m3fn_x4
+ACT = mybir.ActivationFunctionType
+ALU = mybir.AluOpType
+
+P = 128
+MODULES = 8
+ROWS = 512
+FEATURES = 512
+UNITS = 1024
+ROW_TILES = ROWS // P
+HALVES = 2
+HALF_UNITS = UNITS // HALVES
+TILES_PER_HALF = HALF_UNITS // P
+WORDS = FEATURES // 2
+PAIRS = MODULES * HALVES * 2
+STEPS_PER_MODULE = PAIRS // MODULES
+
+SIGMA_MAX = math.exp(4.0)
+SIGMA_MIN = math.exp(-20.0)
+
+HALF_ROWS = MODULES * HALVES
+B11_ROW = 0
+B12_ROW = HALF_ROWS
+EJ_ROW = 2 * HALF_ROWS
+USED_ROWS = 3 * HALF_ROWS
+UNIT_DRAWS = TILES_PER_HALF * HALF_ROWS
+ROW_DRAWS = ROW_TILES * MODULES
+
+LOAD_AHEAD = 2
+
+FLOPS = 2 * 2 * MODULES * ROWS * UNITS * FEATURES
+
+
+def tile_skill_net_pa_t_kernel(tc, s, ei1, ej1, w11, b11, w12, b12, out):
+    nc = tc.nc
+
+    s_view = s.rearrange("(n a) j k -> n a j k", a=ROW_TILES)
+    w_views = [
+        w.rearrange("j (h m c) k -> j h m (c k)", h=HALVES, c=TILES_PER_HALF) for w in (w12, w11)
+    ]
+    out_view = out.rearrange("(n a) j l -> n a j l", a=ROW_TILES)
+
+    with ExitStack() as stack:
+        const = stack.enter_context(tc.tile_pool(name="const", bufs=1))
+        raw = stack.enter_context(tc.tile_pool(name="raw", bufs=4))
+        grouped = stack.enter_context(tc.tile_pool(name="grouped", bufs=3))
+        packed = stack.enter_context(tc.tile_pool(name="packed", bufs=4))
+        work = stack.enter_context(tc.tile_pool(name="work", bufs=3))
+        result = stack.enter_context(tc.tile_pool(name="result", bufs=2))
+        psum = stack.enter_context(tc.psum_pool(name="psum", bufs=2))
+        stack.enter_context(tc.manual_schedule())
+
+        weight_words = {}
+        row_words = {}
+        forward_bank = {}
+        weight_grouped = {}
+        row_grouped = {}
+        weight_codes = {}
+        weight_scales = {}
+        row_codes = {}
+        row_scales = {}
+        row_factor = {}
+        log_sigma_bank = {}
+        mu_bank = {}
+        sigma = {}
+        summed = {}
+        backward_bank = {}
+        out_rows = {}
+
+        def load_rows(j):
+            s_raw = raw.tile([P, ROW_TILES * FEATURES], BF16, name="s_raw", tag="s_raw")
+            nc.sync.dma_start(
+                out=s_raw[:].rearrange("p (a k) -> p a k", a=ROW_TILES), in_=s_view[:, :, j, :]
+            )
+            row_words[j] = s_raw[:].bitcast(F32)
+
+        def load_half(g):
+            w_raw = raw.tile([P, 2 * TILES_PER_HALF * FEATURES], BF16, name="w_raw", tag="w_raw")
+            for x in range(2):
+                nc.sync.dma_start(
+                    out=w_raw[:, x * TILES_PER_HALF * FEATURES : (x + 1) * TILES_PER_HALF * FEATURES],
+                    in_=w_views[x][g // HALVES, g % HALVES],
+                )
+            weight_words[g] = w_raw[:].bitcast(F32)
+
+        def transpose_two_tiles(words, first_word, key):
+            bank = psum.tile([P, 2, 2, P], F32, name="forward", tag="forward")
+            for t in range(2):
+                for u in range(2):
+                    start = first_word + t * WORDS + u * P
+                    nc.tensor.transpose(bank[:, t, u, :], words[:, start : start + P], ident[:])
+            forward_bank[key] = bank
+
+        def side_by_side(key, grouped_words):
+            nc.scalar.copy(
+                out=grouped_words, in_=forward_bank[key][:].rearrange("p t u r -> p t r u")
+            )
+
+        def transpose_weights(q, x):
+            first_word = x * TILES_PER_HALF * WORDS + (q % 2) * 2 * WORDS
+            transpose_two_tiles(weight_words[q // 2], first_word, ("w", q, x))
+
+        def copy_weights(q, x):
+            if x == 0:
+                weight_grouped[q] = grouped.tile(
+                    [P, 4 * P * 4], BF16, name="w_grouped", tag="w_grouped", align_bytes=64
+                )
+            view = weight_grouped[q][:].bitcast(F32).rearrange(
+                "p (x t m u) -> p x t m u", x=2, t=2, u=2
+            )
+            side_by_side(("w", q, x), view[:, x])
+
+        def quantise_weights(q):
+            weight_codes[q] = packed.tile([P, 4 * P], U32, name="w_codes", tag="w_codes", align_bytes=64)
+            weight_scales[q] = packed.tile([P, 4 * P], U8, name="w_scales", tag="w_scales", align_bytes=64)
+            nc.vector.quantize_mx(
+                out=weight_codes[q][:].bitcast(FP8X4),
+                scales=weight_scales[q][:],
+                in_=weight_grouped[q][:],
+            )
+
+        def transpose_rows(j, half):
+            transpose_two_tiles(row_words[j], half * 2 * WORDS, ("s", j, half))
+
+        def copy_rows(j, half):
+            if half == 0:
+                row_grouped[j] = grouped.tile(
+                    [P, ROWS * 4], BF16, name="s_grouped", tag="s_grouped", align_bytes=64
+                )
+            view = row_grouped[j][:].bitcast(F32).rearrange("p (a n u) -> p a n u", a=ROW_TILES, u=2)
+            side_by_side(("s", j, half), view[:, 2 * half : 2 * half + 2])
+
+        def quantise_rows(j):
+            row_codes[j] = packed.tile([P, ROWS], U32, name="s_codes", tag="s_codes", align_bytes=64)
+            row_scales[j] = packed.tile([P, ROWS], U8, name="s_scales", tag="s_scales", align_bytes=64)
+            nc.vector.quantize_mx(
+                out=row_codes[j][:].bitcast(FP8X4),
+                scales=row_scales[j][:],
+                in_=row_grouped[j][:],
+            )
+
+        def spread_row_factor(j):
+            bank = psum.tile([P, ROW_TILES, P], F32, name="forward", tag="forward")
+            for a in range(ROW_TILES):
+                column = UNIT_DRAWS + a * MODULES + j
+                nc.tensor.transpose(
+                    bank[:, a, :], factor[:, column : column + 1].to_broadcast([P, P]), ident[:]
+                )
+            forward_bank[("f", j)] = bank
+
+        def copy_row_factor(j):
+            row_factor[j] = work.tile([P, ROWS], F32, name="row_factor", tag="row_factor")
+            nc.scalar.copy(
+                out=row_factor[j][:], in_=forward_bank[("f", j)][:].rearrange("p a n -> p (a n)")
+            )
+
+        def multiply(q, x, banks, tag):
+            j = q // STEPS_PER_MODULE
+            for t in range(2):
+                bank = psum.tile([P, ROWS], F32, name=tag, tag=tag)
+                columns = slice((2 * x + t) * P, (2 * x + t + 1) * P)
+                nc.tensor.matmul_mx(
+                    out=bank[:],
+                    lhsT=weight_codes[q][:, columns].bitcast(FP8X4),
+                    lhsT_scale=weight_scales[q][:, columns],
+                    rhs=row_codes[j][:].bitcast(FP8X4),
+                    rhs_scale=row_scales[j][:],
+                    start=True,
+                    stop=True,
+                )
+                banks[(q, t)] = bank
+
+        def small(q, t, first_row):
+            return vectors[:, 2 * (q % 2) + t, first_row + q // 2 : first_row + q // 2 + 1]
+
+        def exponentials(q):
+            sigma[q] = work.tile([P, 2, ROWS], F32, name="sigma", tag="sigma")
+            for t in range(2):
+                nc.scalar.activation(
+                    out=sigma[q][:, t, :],
+                    in_=log_sigma_bank[(q, t)][:],
+                    func=ACT.Exp,
+                    bias=small(q, t, B12_ROW),
+                    scale=1.0,
+                )
+
+        def clip_sigma(q):
+            nc.vector.tensor_scalar(
+                out=sigma[q][:],
+                in0=sigma[q][:],
+                scalar1=SIGMA_MAX,
+                scalar2=SIGMA_MIN,
+                op0=ALU.min,
+                op1=ALU.max,
+            )
+
+        def add_noise(q):
+            j = q // STEPS_PER_MODULE
+            if q % 2 == 0:
+                summed[q // 2] = work.tile([P, TILES_PER_HALF, ROWS], F32, name="summed", tag="summed")
+            for t in range(2):
+                c = 2 * (q % 2) + t
+                unit_factor = factor[:, c * HALF_ROWS + q // 2 : c * HALF_ROWS + q // 2 + 1]
+                nc.vector.scalar_tensor_tensor(
+                    out=sigma[q][:, t, :],
+                    in0=sigma[q][:, t, :],
+                    scalar=unit_factor,
+                    in1=row_factor[j][:],
+                    op0=ALU.mult,
+                    op1=ALU.mult,
+                )
+            for t in range(2):
+                nc.vector.scalar_tensor_tensor(
+                    out=summed[q // 2][:, 2 * (q % 2) + t, :],
+                    in0=mu_bank[(q, t)][:],
+                    scalar=small(q, t, B11_ROW),
+                    in1=sigma[q][:, t, :],
+                    op0=ALU.add,
+                    op1=ALU.add,
+                )
+
+        def transpose_back(g, a):
+            bank = psum.tile([P, TILES_PER_HALF, P], F32, name="backward", tag="backward")
+            for c in range(TILES_PER_HALF):
+                nc.tensor.transpose(bank[:, c, :], summed[g][:, c, a * P : (a + 1) * P], ident[:])
+            backward_bank[(g, a)] = bank
+
+        def relu_out(g, a):
+            j, h = g // HALVES, g % HALVES
+            if h == 0 and a == 0:
+                out_rows[j] = result.tile([P, ROW_TILES, UNITS], F32, name="out_rows", tag="out_rows")
+            nc.scalar.activation(
+                out=out_rows[j][:, a, h * HALF_UNITS : (h + 1) * HALF_UNITS].rearrange(
+                    "p (m c) -> p m c", c=TILES_PER_HALF
+                ),
+                in_=backward_bank[(g, a)][:].rearrange("p c m -> p m c"),
+                func=ACT.Relu,
+            )
+
+        def store(j, first_a):
+            nc.gpsimd.dma_start(
+                out=out_view[:, first_a : first_a + 2, j, :], in_=out_rows[j][:, first_a : first_a + 2, :]
+            )
+
+        ident = const.tile([P, P], F32, name="ident")
+        make_identity(nc, ident[:])
+
+        rows_bf16 = const.tile([P, HALF_UNITS], BF16, name="rows_bf16")
+        nc.vector.memset(rows_bf16[:], 0.0)
+        ei_bf16 = const.tile([P, ROW_DRAWS], BF16, name="ei_bf16")
+        nc.sync.dma_start(out=ei_bf16[:], in_=ei1.rearrange("(n a) j o -> n (a j o)", a=ROW_TILES))
+        nc.sync.dma_start(
+            out=rows_bf16[EJ_ROW : EJ_ROW + HALF_ROWS, :],
+            in_=ej1.rearrange("o j (h x) -> (o j h) x", h=HALVES),
+        )
+        nc.sync.dma_start(
+            out=rows_bf16[B12_ROW : B12_ROW + HALF_ROWS, :], in_=b12.rearrange("j (h x) -> (j h) x", h=HALVES)
+        )
+        nc.sync.dma_start(
+            out=rows_bf16[B11_ROW : B11_ROW + HALF_ROWS, :], in_=b11.rearrange("j (h x) -> (j h) x", h=HALVES)
+        )
+        load_rows(0)
+        for g in range(LOAD_AHEAD):
+            load_half(g)
+
+        rows_f32 = const.tile([P, TILES_PER_HALF, P], F32, name="rows_f32")
+        nc.vector.tensor_copy(
+            out=rows_f32[:], in_=rows_bf16[:].rearrange("r (m c) -> r c m", c=TILES_PER_HALF)
+        )
+        vector_bank = psum.tile([P, TILES_PER_HALF, P], F32, name="forward", tag="forward")
+        for c in range(TILES_PER_HALF):
+            nc.tensor.transpose(vector_bank[:, c, :], rows_f32[:, c, :], ident[:])
+        vectors = const.tile([P, TILES_PER_HALF, USED_ROWS], F32, name="vectors")
+        nc.vector.tensor_copy(out=vectors[:], in_=vector_bank[:, :, 0:USED_ROWS])
+
+        draws = const.tile([P, UNIT_DRAWS + ROW_DRAWS], F32, name="draws")
+        nc.vector.tensor_copy(
+            out=draws[:, 0:UNIT_DRAWS].rearrange("p (c r) -> p c r", c=TILES_PER_HALF),
+            in_=vectors[:, :, EJ_ROW : EJ_ROW + HALF_ROWS],
+        )
+        nc.vector.tensor_copy(out=draws[:, UNIT_DRAWS:], in_=ei_bf16[:])
+        magnitude = const.tile([P, UNIT_DRAWS + ROW_DRAWS], F32, name="magnitude")
+        nc.vector.scalar_tensor_tensor(
+            out=magnitude[:], in0=draws[:], scalar=-1.0, in1=draws[:], op0=ALU.mult, op1=ALU.max
+        )
+        root = const.tile([P, UNIT_DRAWS + ROW_DRAWS], F32, name="root")
+        nc.scalar.activation(out=root[:], in_=magnitude[:], func=ACT.Sqrt)
+        signs = const.tile([P, UNIT_DRAWS + ROW_DRAWS], F32, name="signs")
+        nc.scalar.activation(out=signs[:], in_=draws[:], func=ACT.Sign)
+        factor = const.tile([P, UNIT_DRAWS + ROW_DRAWS], F32, name="factor")
+        nc.vector.tensor_mul(out=factor[:], in0=signs[:], in1=root[:])
+
+        for q in range(-4, PAIRS + 3):
+            phase = q % STEPS_PER_MODULE
+            coming = q // STEPS_PER_MODULE + 1
+
+            if q % 2 == 0:
+                g = (q + 4) // 2 + LOAD_AHEAD
+                if g < MODULES * HALVES:
+                    if g % HALVES == 0:
+                        load_rows(g // HALVES)
+                    load_half(g)
+
+            if 0 <= q < PAIRS:
+                exponentials(q)
+            if 0 <= q + 1 < PAIRS:
+                multiply(q + 1, 0, log_sigma_bank, "log_sigma")
+            if 0 <= q < PAIRS:
+                multiply(q, 1, mu_bank, "mu")
+
+            for i in range(2):
+                if 0 <= q - 3 < PAIRS:
+                    relu_out((q - 3) // 2, 2 * ((q - 3) % 2) + i)
+                if 0 <= q - 2 < PAIRS:
+                    transpose_back((q - 2) // 2, 2 * ((q - 2) % 2) + i)
+            if 0 <= q - 3 < PAIRS and ((q - 3) // 2) % HALVES == 1:
+                store((q - 3) // STEPS_PER_MODULE, 2 * ((q - 3) % 2))
+
+            extra = coming < MODULES and phase < 3
+            if 0 <= q + 3 < PAIRS:
+                copy_weights(q + 3, 0)
+            if extra and phase < 2:
+                transpose_rows(coming, phase)
+            if extra and phase == 2:
+                spread_row_factor(coming)
+            if 0 <= q + 3 < PAIRS:
+                copy_weights(q + 3, 1)
+            if q + 4 < PAIRS:
+                transpose_weights(q + 4, 0)
+            if extra and phase < 2:
+                copy_rows(coming, phase)
+            if extra and phase == 2:
+                copy_row_factor(coming)
+            if q + 4 < PAIRS:
+                transpose_weights(q + 4, 1)
+
+            if 0 <= q < PAIRS:
+                clip_sigma(q)
+            if 0 <= q + 2 < PAIRS:
+                quantise_weights(q + 2)
+            if extra and phase == 2:
+                quantise_rows(coming)
+            if 0 <= q < PAIRS:
+                add_noise(q)

@@ -36,7 +36,7 @@ USED_ROWS = 3 * HALF_ROWS
 UNIT_DRAWS = TILES_PER_HALF * HALF_ROWS
 ROW_DRAWS = ROW_TILES * MODULES
 
-LOAD_AHEAD = 2
+LOAD_AHEAD = 3
 
 FLOPS = 2 * 2 * MODULES * ROWS * UNITS * FEATURES
 
@@ -52,7 +52,7 @@ def tile_skill_net_pa_t_kernel(tc, s, ei1, ej1, w11, b11, w12, b12, out):
 
     with ExitStack() as stack:
         const = stack.enter_context(tc.tile_pool(name="const", bufs=1))
-        raw = stack.enter_context(tc.tile_pool(name="raw", bufs=4))
+        raw = stack.enter_context(tc.tile_pool(name="raw", bufs=LOAD_AHEAD + 2))
         grouped = stack.enter_context(tc.tile_pool(name="grouped", bufs=3))
         packed = stack.enter_context(tc.tile_pool(name="packed", bufs=4))
         work = stack.enter_context(tc.tile_pool(name="work", bufs=3))
@@ -101,10 +101,8 @@ def tile_skill_net_pa_t_kernel(tc, s, ei1, ej1, w11, b11, w12, b12, out):
                     nc.tensor.transpose(bank[:, t, u, :], words[:, start : start + P], ident[:])
             forward_bank[key] = bank
 
-        def side_by_side(key, grouped_words):
-            nc.scalar.copy(
-                out=grouped_words, in_=forward_bank[key][:].rearrange("p t u r -> p t r u")
-            )
+        def side_by_side(copy, key, grouped_words):
+            copy(out=grouped_words, in_=forward_bank[key][:].rearrange("p t u r -> p t r u"))
 
         def transpose_weights(q, x):
             first_word = x * TILES_PER_HALF * WORDS + (q % 2) * 2 * WORDS
@@ -118,7 +116,7 @@ def tile_skill_net_pa_t_kernel(tc, s, ei1, ej1, w11, b11, w12, b12, out):
             view = weight_grouped[q][:].bitcast(F32).rearrange(
                 "p (x t m u) -> p x t m u", x=2, t=2, u=2
             )
-            side_by_side(("w", q, x), view[:, x])
+            side_by_side(nc.scalar.copy, ("w", q, x), view[:, x])
 
         def quantise_weights(q):
             weight_codes[q] = packed.tile([P, 4 * P], U32, name="w_codes", tag="w_codes", align_bytes=64)
@@ -138,7 +136,7 @@ def tile_skill_net_pa_t_kernel(tc, s, ei1, ej1, w11, b11, w12, b12, out):
                     [P, ROWS * 4], BF16, name="s_grouped", tag="s_grouped", align_bytes=64
                 )
             view = row_grouped[j][:].bitcast(F32).rearrange("p (a n u) -> p a n u", a=ROW_TILES, u=2)
-            side_by_side(("s", j, half), view[:, 2 * half : 2 * half + 2])
+            side_by_side(nc.vector.tensor_copy, ("s", j, half), view[:, 2 * half : 2 * half + 2])
 
         def quantise_rows(j):
             row_codes[j] = packed.tile([P, ROWS], U32, name="s_codes", tag="s_codes", align_bytes=64)
@@ -160,7 +158,7 @@ def tile_skill_net_pa_t_kernel(tc, s, ei1, ej1, w11, b11, w12, b12, out):
 
         def copy_row_factor(j):
             row_factor[j] = work.tile([P, ROWS], F32, name="row_factor", tag="row_factor")
-            nc.scalar.copy(
+            nc.vector.tensor_copy(
                 out=row_factor[j][:], in_=forward_bank[("f", j)][:].rearrange("p a n -> p (a n)")
             )
 
@@ -195,19 +193,18 @@ def tile_skill_net_pa_t_kernel(tc, s, ei1, ej1, w11, b11, w12, b12, out):
                 )
 
         def clip_sigma(q):
-            nc.vector.tensor_scalar(
-                out=sigma[q][:],
-                in0=sigma[q][:],
-                scalar1=SIGMA_MAX,
-                scalar2=SIGMA_MIN,
-                op0=ALU.min,
-                op1=ALU.max,
-            )
+            for t in range(2):
+                nc.gpsimd.tensor_scalar(
+                    out=sigma[q][:, t, :],
+                    in0=sigma[q][:, t, :],
+                    scalar1=SIGMA_MAX,
+                    scalar2=SIGMA_MIN,
+                    op0=ALU.min,
+                    op1=ALU.max,
+                )
 
-        def add_noise(q):
+        def scale_noise(q):
             j = q // STEPS_PER_MODULE
-            if q % 2 == 0:
-                summed[q // 2] = work.tile([P, TILES_PER_HALF, ROWS], F32, name="summed", tag="summed")
             for t in range(2):
                 c = 2 * (q % 2) + t
                 unit_factor = factor[:, c * HALF_ROWS + q // 2 : c * HALF_ROWS + q // 2 + 1]
@@ -219,6 +216,10 @@ def tile_skill_net_pa_t_kernel(tc, s, ei1, ej1, w11, b11, w12, b12, out):
                     op0=ALU.mult,
                     op1=ALU.mult,
                 )
+
+        def add_mu(q):
+            if q % 2 == 0:
+                summed[q // 2] = work.tile([P, TILES_PER_HALF, ROWS], F32, name="summed", tag="summed")
             for t in range(2):
                 nc.vector.scalar_tensor_tensor(
                     out=summed[q // 2][:, 2 * (q % 2) + t, :],
@@ -248,7 +249,7 @@ def tile_skill_net_pa_t_kernel(tc, s, ei1, ej1, w11, b11, w12, b12, out):
             )
 
         def store(j, first_a):
-            nc.gpsimd.dma_start(
+            nc.sync.dma_start(
                 out=out_view[:, first_a : first_a + 2, j, :], in_=out_rows[j][:, first_a : first_a + 2, :]
             )
 
@@ -269,8 +270,9 @@ def tile_skill_net_pa_t_kernel(tc, s, ei1, ej1, w11, b11, w12, b12, out):
         nc.sync.dma_start(
             out=rows_bf16[B11_ROW : B11_ROW + HALF_ROWS, :], in_=b11.rearrange("j (h x) -> (j h) x", h=HALVES)
         )
-        load_rows(0)
         for g in range(LOAD_AHEAD):
+            if g % HALVES == 0:
+                load_rows(g // HALVES)
             load_half(g)
 
         rows_f32 = const.tile([P, TILES_PER_HALF, P], F32, name="rows_f32")
@@ -303,6 +305,9 @@ def tile_skill_net_pa_t_kernel(tc, s, ei1, ej1, w11, b11, w12, b12, out):
         for q in range(-4, PAIRS + 3):
             phase = q % STEPS_PER_MODULE
             coming = q // STEPS_PER_MODULE + 1
+            extra_rows = coming < MODULES and phase < 2
+            extra_factor = coming < MODULES and phase == 2
+            ending = q - 3
 
             if q % 2 == 0:
                 g = (q + 4) // 2 + LOAD_AHEAD
@@ -313,42 +318,44 @@ def tile_skill_net_pa_t_kernel(tc, s, ei1, ej1, w11, b11, w12, b12, out):
 
             if 0 <= q < PAIRS:
                 exponentials(q)
+                clip_sigma(q)
             if 0 <= q + 1 < PAIRS:
                 multiply(q + 1, 0, log_sigma_bank, "log_sigma")
             if 0 <= q < PAIRS:
                 multiply(q, 1, mu_bank, "mu")
 
-            for i in range(2):
-                if 0 <= q - 3 < PAIRS:
-                    relu_out((q - 3) // 2, 2 * ((q - 3) % 2) + i)
-                if 0 <= q - 2 < PAIRS:
-                    transpose_back((q - 2) // 2, 2 * ((q - 2) % 2) + i)
-            if 0 <= q - 3 < PAIRS and ((q - 3) // 2) % HALVES == 1:
-                store((q - 3) // STEPS_PER_MODULE, 2 * ((q - 3) % 2))
-
-            extra = coming < MODULES and phase < 3
             if 0 <= q + 3 < PAIRS:
                 copy_weights(q + 3, 0)
-            if extra and phase < 2:
+            if extra_rows:
                 transpose_rows(coming, phase)
-            if extra and phase == 2:
+            if extra_factor:
                 spread_row_factor(coming)
+            if 0 <= ending < PAIRS:
+                relu_out(ending // 2, 2 * (ending % 2))
+            if 0 <= q - 2 < PAIRS:
+                transpose_back((q - 2) // 2, 2 * ((q - 2) % 2))
             if 0 <= q + 3 < PAIRS:
                 copy_weights(q + 3, 1)
             if q + 4 < PAIRS:
                 transpose_weights(q + 4, 0)
-            if extra and phase < 2:
+            if 0 <= ending < PAIRS:
+                relu_out(ending // 2, 2 * (ending % 2) + 1)
+            if 0 <= q - 2 < PAIRS:
+                transpose_back((q - 2) // 2, 2 * ((q - 2) % 2) + 1)
+            if 0 <= ending < PAIRS and (ending // 2) % HALVES == 1:
+                store(ending // STEPS_PER_MODULE, 2 * (ending % 2))
+
+            if 0 <= q + 2 < PAIRS:
+                quantise_weights(q + 2)
+            if extra_factor:
+                quantise_rows(coming)
+            if 0 <= q < PAIRS:
+                scale_noise(q)
+            if extra_rows:
                 copy_rows(coming, phase)
-            if extra and phase == 2:
+            if extra_factor:
                 copy_row_factor(coming)
             if q + 4 < PAIRS:
                 transpose_weights(q + 4, 1)
-
             if 0 <= q < PAIRS:
-                clip_sigma(q)
-            if 0 <= q + 2 < PAIRS:
-                quantise_weights(q + 2)
-            if extra and phase == 2:
-                quantise_rows(coming)
-            if 0 <= q < PAIRS:
-                add_noise(q)
+                add_mu(q)

@@ -18,25 +18,18 @@ ROWS = 512
 FEATURES = 512
 UNITS = 1024
 ROW_TILES = ROWS // P
-HALVES = 2
-HALF_UNITS = UNITS // HALVES
-TILES_PER_HALF = HALF_UNITS // P
+UNIT_TILES = UNITS // P
 WORDS = FEATURES // 2
-PAIRS = MODULES * HALVES * 2
-STEPS_PER_MODULE = PAIRS // MODULES
+STEPS_PER_MODULE = UNIT_TILES // 2
+PAIRS = MODULES * STEPS_PER_MODULE
 
 SIGMA_MAX = math.exp(4.0)
 SIGMA_MIN = math.exp(-20.0)
 
-HALF_ROWS = MODULES * HALVES
-B11_ROW = 0
-B12_ROW = HALF_ROWS
-EJ_ROW = 2 * HALF_ROWS
-USED_ROWS = 3 * HALF_ROWS
-UNIT_DRAWS = TILES_PER_HALF * HALF_ROWS
+TILE_ROWS = MODULES * UNIT_TILES
 ROW_DRAWS = ROW_TILES * MODULES
 
-LOAD_AHEAD = 3
+LOAD_AHEAD = 6
 
 FLOPS = 2 * 2 * MODULES * ROWS * UNITS * FEATURES
 
@@ -45,18 +38,17 @@ def tile_skill_net_pa_t_kernel(tc, s, ei1, ej1, w11, b11, w12, b12, out):
     nc = tc.nc
 
     s_view = s.rearrange("(n a) j k -> n a j k", a=ROW_TILES)
-    w_views = [
-        w.rearrange("j (h m c) k -> j h m (c k)", h=HALVES, c=TILES_PER_HALF) for w in (w12, w11)
-    ]
+    w_views = [w.rearrange("j (t m) k -> j m t k", m=P) for w in (w12, w11)]
     out_view = out.rearrange("(n a) j l -> n a j l", a=ROW_TILES)
 
     with ExitStack() as stack:
         const = stack.enter_context(tc.tile_pool(name="const", bufs=1))
-        raw = stack.enter_context(tc.tile_pool(name="raw", bufs=LOAD_AHEAD + 2))
+        raw_weights = stack.enter_context(tc.tile_pool(name="raw_weights", bufs=LOAD_AHEAD + 2))
+        raw_rows = stack.enter_context(tc.tile_pool(name="raw_rows", bufs=3))
         grouped = stack.enter_context(tc.tile_pool(name="grouped", bufs=3))
         packed = stack.enter_context(tc.tile_pool(name="packed", bufs=4))
         work = stack.enter_context(tc.tile_pool(name="work", bufs=3))
-        result = stack.enter_context(tc.tile_pool(name="result", bufs=2))
+        result = stack.enter_context(tc.tile_pool(name="result", bufs=4))
         psum = stack.enter_context(tc.psum_pool(name="psum", bufs=2))
         stack.enter_context(tc.manual_schedule())
 
@@ -75,23 +67,31 @@ def tile_skill_net_pa_t_kernel(tc, s, ei1, ej1, w11, b11, w12, b12, out):
         sigma = {}
         summed = {}
         backward_bank = {}
-        out_rows = {}
+        out_pair = {}
 
         def load_rows(j):
-            s_raw = raw.tile([P, ROW_TILES * FEATURES], BF16, name="s_raw", tag="s_raw")
+            s_raw = raw_rows.tile([P, ROW_TILES * FEATURES], BF16, name="s_raw")
             nc.sync.dma_start(
                 out=s_raw[:].rearrange("p (a k) -> p a k", a=ROW_TILES), in_=s_view[:, :, j, :]
             )
             row_words[j] = s_raw[:].bitcast(F32)
 
-        def load_half(g):
-            w_raw = raw.tile([P, 2 * TILES_PER_HALF * FEATURES], BF16, name="w_raw", tag="w_raw")
+        def load_weights(q):
+            j, first_tile = q // STEPS_PER_MODULE, 2 * (q % STEPS_PER_MODULE)
+            w_raw = raw_weights.tile([P, 2 * 2 * FEATURES], BF16, name="w_raw")
             for x in range(2):
                 nc.sync.dma_start(
-                    out=w_raw[:, x * TILES_PER_HALF * FEATURES : (x + 1) * TILES_PER_HALF * FEATURES],
-                    in_=w_views[x][g // HALVES, g % HALVES],
+                    out=w_raw[:, x * 2 * FEATURES : (x + 1) * 2 * FEATURES].rearrange(
+                        "p (t k) -> p t k", t=2
+                    ),
+                    in_=w_views[x][j, :, first_tile : first_tile + 2, :],
                 )
-            weight_words[g] = w_raw[:].bitcast(F32)
+            weight_words[q] = w_raw[:].bitcast(F32)
+
+        def load_for_pair(q):
+            if q % STEPS_PER_MODULE == 0:
+                load_rows(q // STEPS_PER_MODULE)
+            load_weights(q)
 
         def transpose_two_tiles(words, first_word, key):
             bank = psum.tile([P, 2, 2, P], F32, name="forward", tag="forward")
@@ -105,22 +105,19 @@ def tile_skill_net_pa_t_kernel(tc, s, ei1, ej1, w11, b11, w12, b12, out):
             copy(out=grouped_words, in_=forward_bank[key][:].rearrange("p t u r -> p t r u"))
 
         def transpose_weights(q, x):
-            first_word = x * TILES_PER_HALF * WORDS + (q % 2) * 2 * WORDS
-            transpose_two_tiles(weight_words[q // 2], first_word, ("w", q, x))
+            transpose_two_tiles(weight_words[q], x * 2 * WORDS, ("w", q, x))
 
         def copy_weights(q, x):
             if x == 0:
-                weight_grouped[q] = grouped.tile(
-                    [P, 4 * P * 4], BF16, name="w_grouped", tag="w_grouped", align_bytes=64
-                )
+                weight_grouped[q] = grouped.tile([P, 4 * P * 4], BF16, name="w_grouped", align_bytes=64)
             view = weight_grouped[q][:].bitcast(F32).rearrange(
                 "p (x t m u) -> p x t m u", x=2, t=2, u=2
             )
             side_by_side(nc.scalar.copy, ("w", q, x), view[:, x])
 
         def quantise_weights(q):
-            weight_codes[q] = packed.tile([P, 4 * P], U32, name="w_codes", tag="w_codes", align_bytes=64)
-            weight_scales[q] = packed.tile([P, 4 * P], U8, name="w_scales", tag="w_scales", align_bytes=64)
+            weight_codes[q] = packed.tile([P, 4 * P], U32, name="w_codes", align_bytes=64)
+            weight_scales[q] = packed.tile([P, 4 * P], U8, name="w_scales", align_bytes=64)
             nc.vector.quantize_mx(
                 out=weight_codes[q][:].bitcast(FP8X4),
                 scales=weight_scales[q][:],
@@ -132,15 +129,13 @@ def tile_skill_net_pa_t_kernel(tc, s, ei1, ej1, w11, b11, w12, b12, out):
 
         def copy_rows(j, half):
             if half == 0:
-                row_grouped[j] = grouped.tile(
-                    [P, ROWS * 4], BF16, name="s_grouped", tag="s_grouped", align_bytes=64
-                )
+                row_grouped[j] = grouped.tile([P, ROWS * 4], BF16, name="s_grouped", align_bytes=64)
             view = row_grouped[j][:].bitcast(F32).rearrange("p (a n u) -> p a n u", a=ROW_TILES, u=2)
             side_by_side(nc.vector.tensor_copy, ("s", j, half), view[:, 2 * half : 2 * half + 2])
 
         def quantise_rows(j):
-            row_codes[j] = packed.tile([P, ROWS], U32, name="s_codes", tag="s_codes", align_bytes=64)
-            row_scales[j] = packed.tile([P, ROWS], U8, name="s_scales", tag="s_scales", align_bytes=64)
+            row_codes[j] = packed.tile([P, ROWS], U32, name="s_codes", align_bytes=64)
+            row_scales[j] = packed.tile([P, ROWS], U8, name="s_scales", align_bytes=64)
             nc.vector.quantize_mx(
                 out=row_codes[j][:].bitcast(FP8X4),
                 scales=row_scales[j][:],
@@ -150,14 +145,14 @@ def tile_skill_net_pa_t_kernel(tc, s, ei1, ej1, w11, b11, w12, b12, out):
         def spread_row_factor(j):
             bank = psum.tile([P, ROW_TILES, P], F32, name="forward", tag="forward")
             for a in range(ROW_TILES):
-                column = UNIT_DRAWS + a * MODULES + j
+                column = TILE_ROWS + a * MODULES + j
                 nc.tensor.transpose(
                     bank[:, a, :], factor[:, column : column + 1].to_broadcast([P, P]), ident[:]
                 )
             forward_bank[("f", j)] = bank
 
         def copy_row_factor(j):
-            row_factor[j] = work.tile([P, ROWS], F32, name="row_factor", tag="row_factor")
+            row_factor[j] = work.tile([P, ROWS], F32, name="row_factor")
             nc.vector.tensor_copy(
                 out=row_factor[j][:], in_=forward_bank[("f", j)][:].rearrange("p a n -> p (a n)")
             )
@@ -178,17 +173,14 @@ def tile_skill_net_pa_t_kernel(tc, s, ei1, ej1, w11, b11, w12, b12, out):
                 )
                 banks[(q, t)] = bank
 
-        def small(q, t, first_row):
-            return vectors[:, 2 * (q % 2) + t, first_row + q // 2 : first_row + q // 2 + 1]
-
         def exponentials(q):
-            sigma[q] = work.tile([P, 2, ROWS], F32, name="sigma", tag="sigma")
+            sigma[q] = work.tile([P, 2, ROWS], F32, name="sigma")
             for t in range(2):
                 nc.scalar.activation(
                     out=sigma[q][:, t, :],
                     in_=log_sigma_bank[(q, t)][:],
                     func=ACT.Exp,
-                    bias=small(q, t, B12_ROW),
+                    bias=b12_columns[:, 2 * q + t : 2 * q + t + 1],
                     scale=1.0,
                 )
 
@@ -204,117 +196,95 @@ def tile_skill_net_pa_t_kernel(tc, s, ei1, ej1, w11, b11, w12, b12, out):
                 )
 
         def scale_noise(q):
-            j = q // STEPS_PER_MODULE
             for t in range(2):
-                c = 2 * (q % 2) + t
-                unit_factor = factor[:, c * HALF_ROWS + q // 2 : c * HALF_ROWS + q // 2 + 1]
                 nc.vector.scalar_tensor_tensor(
                     out=sigma[q][:, t, :],
                     in0=sigma[q][:, t, :],
-                    scalar=unit_factor,
-                    in1=row_factor[j][:],
+                    scalar=factor[:, 2 * q + t : 2 * q + t + 1],
+                    in1=row_factor[q // STEPS_PER_MODULE][:],
                     op0=ALU.mult,
                     op1=ALU.mult,
                 )
 
         def add_mu(q):
-            if q % 2 == 0:
-                summed[q // 2] = work.tile([P, TILES_PER_HALF, ROWS], F32, name="summed", tag="summed")
+            summed[q] = work.tile([P, 2, ROWS], F32, name="summed")
             for t in range(2):
                 nc.vector.scalar_tensor_tensor(
-                    out=summed[q // 2][:, 2 * (q % 2) + t, :],
+                    out=summed[q][:, t, :],
                     in0=mu_bank[(q, t)][:],
-                    scalar=small(q, t, B11_ROW),
+                    scalar=b11_columns[:, 2 * q + t : 2 * q + t + 1],
                     in1=sigma[q][:, t, :],
                     op0=ALU.add,
                     op1=ALU.add,
                 )
 
-        def transpose_back(g, a):
-            bank = psum.tile([P, TILES_PER_HALF, P], F32, name="backward", tag="backward")
-            for c in range(TILES_PER_HALF):
-                nc.tensor.transpose(bank[:, c, :], summed[g][:, c, a * P : (a + 1) * P], ident[:])
-            backward_bank[(g, a)] = bank
+        def transpose_back(q, t):
+            bank = psum.tile([P, ROW_TILES, P], F32, name="backward", tag="backward")
+            for a in range(ROW_TILES):
+                nc.tensor.transpose(bank[:, a, :], summed[q][:, t, a * P : (a + 1) * P], ident[:])
+            backward_bank[(q, t)] = bank
 
-        def relu_out(g, a):
-            j, h = g // HALVES, g % HALVES
-            if h == 0 and a == 0:
-                out_rows[j] = result.tile([P, ROW_TILES, UNITS], F32, name="out_rows", tag="out_rows")
-            nc.scalar.activation(
-                out=out_rows[j][:, a, h * HALF_UNITS : (h + 1) * HALF_UNITS].rearrange(
-                    "p (m c) -> p m c", c=TILES_PER_HALF
-                ),
-                in_=backward_bank[(g, a)][:].rearrange("p c m -> p m c"),
-                func=ACT.Relu,
-            )
+        def relu_out(q, t, on_vector):
+            if t == 0:
+                out_pair[q] = result.tile([P, ROW_TILES, 2 * P], F32, name="out_pair")
+            columns = out_pair[q][:, :, t * P : (t + 1) * P]
+            if on_vector:
+                nc.vector.tensor_scalar_max(out=columns, in0=backward_bank[(q, t)][:], scalar1=0.0)
+            else:
+                nc.scalar.activation(out=columns, in_=backward_bank[(q, t)][:], func=ACT.Relu)
 
-        def store(j, first_a):
+        def store(q):
+            j, first_unit = q // STEPS_PER_MODULE, 2 * P * (q % STEPS_PER_MODULE)
             nc.sync.dma_start(
-                out=out_view[:, first_a : first_a + 2, j, :], in_=out_rows[j][:, first_a : first_a + 2, :]
+                out=out_view[:, :, j, first_unit : first_unit + 2 * P], in_=out_pair[q][:]
             )
 
         ident = const.tile([P, P], F32, name="ident")
         make_identity(nc, ident[:])
 
-        rows_bf16 = const.tile([P, HALF_UNITS], BF16, name="rows_bf16")
+        rows_bf16 = const.tile([P, 2, P], BF16, name="rows_bf16")
         nc.vector.memset(rows_bf16[:], 0.0)
         ei_bf16 = const.tile([P, ROW_DRAWS], BF16, name="ei_bf16")
         nc.sync.dma_start(out=ei_bf16[:], in_=ei1.rearrange("(n a) j o -> n (a j o)", a=ROW_TILES))
-        nc.sync.dma_start(
-            out=rows_bf16[EJ_ROW : EJ_ROW + HALF_ROWS, :],
-            in_=ej1.rearrange("o j (h x) -> (o j h) x", h=HALVES),
-        )
-        nc.sync.dma_start(
-            out=rows_bf16[B12_ROW : B12_ROW + HALF_ROWS, :], in_=b12.rearrange("j (h x) -> (j h) x", h=HALVES)
-        )
-        nc.sync.dma_start(
-            out=rows_bf16[B11_ROW : B11_ROW + HALF_ROWS, :], in_=b11.rearrange("j (h x) -> (j h) x", h=HALVES)
-        )
-        for g in range(LOAD_AHEAD):
-            if g % HALVES == 0:
-                load_rows(g // HALVES)
-            load_half(g)
+        nc.sync.dma_start(out=rows_bf16[0:TILE_ROWS, 1, :], in_=ej1.rearrange("o j (t m) -> (o j t) m", m=P))
+        nc.sync.dma_start(out=rows_bf16[0:TILE_ROWS, 0, :], in_=b11.rearrange("j (t m) -> (j t) m", m=P))
+        nc.sync.dma_start(out=rows_bf16[TILE_ROWS:P, 0, :], in_=b12.rearrange("j (t m) -> (j t) m", m=P))
+        for q in range(LOAD_AHEAD):
+            load_for_pair(q)
 
-        rows_f32 = const.tile([P, TILES_PER_HALF, P], F32, name="rows_f32")
-        nc.vector.tensor_copy(
-            out=rows_f32[:], in_=rows_bf16[:].rearrange("r (m c) -> r c m", c=TILES_PER_HALF)
-        )
-        vector_bank = psum.tile([P, TILES_PER_HALF, P], F32, name="forward", tag="forward")
-        for c in range(TILES_PER_HALF):
-            nc.tensor.transpose(vector_bank[:, c, :], rows_f32[:, c, :], ident[:])
-        vectors = const.tile([P, TILES_PER_HALF, USED_ROWS], F32, name="vectors")
-        nc.vector.tensor_copy(out=vectors[:], in_=vector_bank[:, :, 0:USED_ROWS])
+        rows_f32 = const.tile([P, 2, P], F32, name="rows_f32")
+        nc.vector.tensor_copy(out=rows_f32[:], in_=rows_bf16[:])
+        vector_bank = psum.tile([P, 2, P], F32, name="forward", tag="forward")
+        for plane in range(2):
+            nc.tensor.transpose(vector_bank[:, plane, :], rows_f32[:, plane, :], ident[:])
+        b11_columns = const.tile([P, TILE_ROWS], F32, name="b11_columns")
+        nc.vector.tensor_copy(out=b11_columns[:], in_=vector_bank[:, 0, 0:TILE_ROWS])
+        b12_columns = const.tile([P, TILE_ROWS], F32, name="b12_columns")
+        nc.vector.tensor_copy(out=b12_columns[:], in_=vector_bank[:, 0, TILE_ROWS:P])
 
-        draws = const.tile([P, UNIT_DRAWS + ROW_DRAWS], F32, name="draws")
-        nc.vector.tensor_copy(
-            out=draws[:, 0:UNIT_DRAWS].rearrange("p (c r) -> p c r", c=TILES_PER_HALF),
-            in_=vectors[:, :, EJ_ROW : EJ_ROW + HALF_ROWS],
-        )
-        nc.vector.tensor_copy(out=draws[:, UNIT_DRAWS:], in_=ei_bf16[:])
-        magnitude = const.tile([P, UNIT_DRAWS + ROW_DRAWS], F32, name="magnitude")
+        draws = const.tile([P, TILE_ROWS + ROW_DRAWS], F32, name="draws")
+        nc.vector.tensor_copy(out=draws[:, 0:TILE_ROWS], in_=vector_bank[:, 1, 0:TILE_ROWS])
+        nc.vector.tensor_copy(out=draws[:, TILE_ROWS:], in_=ei_bf16[:])
+        magnitude = const.tile([P, TILE_ROWS + ROW_DRAWS], F32, name="magnitude")
         nc.vector.scalar_tensor_tensor(
             out=magnitude[:], in0=draws[:], scalar=-1.0, in1=draws[:], op0=ALU.mult, op1=ALU.max
         )
-        root = const.tile([P, UNIT_DRAWS + ROW_DRAWS], F32, name="root")
+        root = const.tile([P, TILE_ROWS + ROW_DRAWS], F32, name="root")
         nc.scalar.activation(out=root[:], in_=magnitude[:], func=ACT.Sqrt)
-        signs = const.tile([P, UNIT_DRAWS + ROW_DRAWS], F32, name="signs")
+        signs = const.tile([P, TILE_ROWS + ROW_DRAWS], F32, name="signs")
         nc.scalar.activation(out=signs[:], in_=draws[:], func=ACT.Sign)
-        factor = const.tile([P, UNIT_DRAWS + ROW_DRAWS], F32, name="factor")
+        factor = const.tile([P, TILE_ROWS + ROW_DRAWS], F32, name="factor")
         nc.vector.tensor_mul(out=factor[:], in0=signs[:], in1=root[:])
 
-        for q in range(-4, PAIRS + 3):
+        for q in range(-4, PAIRS + 2):
             phase = q % STEPS_PER_MODULE
             coming = q // STEPS_PER_MODULE + 1
             extra_rows = coming < MODULES and phase < 2
             extra_factor = coming < MODULES and phase == 2
-            ending = q - 3
+            vector_is_done = q >= PAIRS
 
-            if q % 2 == 0:
-                g = (q + 4) // 2 + LOAD_AHEAD
-                if g < MODULES * HALVES:
-                    if g % HALVES == 0:
-                        load_rows(g // HALVES)
-                    load_half(g)
+            if q + 4 + LOAD_AHEAD < PAIRS:
+                load_for_pair(q + 4 + LOAD_AHEAD)
 
             if 0 <= q < PAIRS:
                 exponentials(q)
@@ -330,20 +300,19 @@ def tile_skill_net_pa_t_kernel(tc, s, ei1, ej1, w11, b11, w12, b12, out):
                 transpose_rows(coming, phase)
             if extra_factor:
                 spread_row_factor(coming)
-            if 0 <= ending < PAIRS:
-                relu_out(ending // 2, 2 * (ending % 2))
             if 0 <= q - 2 < PAIRS:
-                transpose_back((q - 2) // 2, 2 * ((q - 2) % 2))
+                relu_out(q - 2, 0, False)
+            if 0 <= q - 1 < PAIRS:
+                transpose_back(q - 1, 0)
             if 0 <= q + 3 < PAIRS:
                 copy_weights(q + 3, 1)
             if q + 4 < PAIRS:
                 transpose_weights(q + 4, 0)
-            if 0 <= ending < PAIRS:
-                relu_out(ending // 2, 2 * (ending % 2) + 1)
             if 0 <= q - 2 < PAIRS:
-                transpose_back((q - 2) // 2, 2 * ((q - 2) % 2) + 1)
-            if 0 <= ending < PAIRS and (ending // 2) % HALVES == 1:
-                store(ending // STEPS_PER_MODULE, 2 * (ending % 2))
+                relu_out(q - 2, 1, vector_is_done)
+                store(q - 2)
+            if 0 <= q - 1 < PAIRS:
+                transpose_back(q - 1, 1)
 
             if 0 <= q + 2 < PAIRS:
                 quantise_weights(q + 2)

@@ -280,7 +280,7 @@ def tile_skill_net_pa_t_kernel(tc, s, ei1, ej1, w11, b11, w12, b12, out):
             phase = q % STEPS_PER_MODULE
             coming = q // STEPS_PER_MODULE + 1
             extra_rows = coming < MODULES and phase < 2
-            extra_factor = coming < MODULES and phase == 2
+            extra_factor = coming < MODULES and phase == 3
             vector_is_done = q >= PAIRS
 
             if q + 4 + LOAD_AHEAD < PAIRS:
@@ -291,8 +291,6 @@ def tile_skill_net_pa_t_kernel(tc, s, ei1, ej1, w11, b11, w12, b12, out):
                 clip_sigma(q)
             if 0 <= q + 1 < PAIRS:
                 multiply(q + 1, 0, log_sigma_bank, "log_sigma")
-            if 0 <= q < PAIRS:
-                multiply(q, 1, mu_bank, "mu")
 
             if 0 <= q + 3 < PAIRS:
                 copy_weights(q + 3, 0)
@@ -308,6 +306,10 @@ def tile_skill_net_pa_t_kernel(tc, s, ei1, ej1, w11, b11, w12, b12, out):
                 copy_weights(q + 3, 1)
             if q + 4 < PAIRS:
                 transpose_weights(q + 4, 0)
+
+            if 0 <= q < PAIRS:
+                multiply(q, 1, mu_bank, "mu")
+
             if 0 <= q - 2 < PAIRS:
                 relu_out(q - 2, 1, vector_is_done)
                 store(q - 2)
@@ -316,7 +318,7 @@ def tile_skill_net_pa_t_kernel(tc, s, ei1, ej1, w11, b11, w12, b12, out):
 
             if 0 <= q + 2 < PAIRS:
                 quantise_weights(q + 2)
-            if extra_factor:
+            if coming < MODULES and phase == 2:
                 quantise_rows(coming)
             if 0 <= q < PAIRS:
                 scale_noise(q)

@@ -13,6 +13,7 @@ ACT = mybir.ActivationFunctionType
 ALU = mybir.AluOpType
 
 P = 128
+PACK = 4
 MODULES = 8
 ROWS = 512
 FEATURES = 512
@@ -25,10 +26,16 @@ PAIRS = MODULES * STEPS_PER_MODULE
 
 SIGMA_MAX = math.exp(4.0)
 SIGMA_MIN = math.exp(-20.0)
+SQRT_MIN = 2.0**-116
 
-TILE_ROWS = MODULES * UNIT_TILES
-ROW_DRAWS = ROW_TILES * MODULES
+UNIT_COLUMNS = MODULES * UNIT_TILES
+ROW_COLUMNS = ROW_TILES * MODULES
 
+TRANSPOSE_AHEAD = 4
+COPY_AHEAD = 3
+QUANTISE_AHEAD = 2
+BACK_BEHIND = 1
+RELU_BEHIND = 2
 LOAD_AHEAD = 6
 
 FLOPS = 2 * 2 * MODULES * ROWS * UNITS * FEATURES
@@ -38,7 +45,7 @@ def tile_skill_net_pa_t_kernel(tc, s, ei1, ej1, w11, b11, w12, b12, out):
     nc = tc.nc
 
     s_view = s.rearrange("(n a) j k -> n a j k", a=ROW_TILES)
-    w_views = [w.rearrange("j (t m) k -> j m t k", m=P) for w in (w12, w11)]
+    w_views = [w.rearrange("j (g m) k -> j m g k", m=P) for w in (w12, w11)]
     out_view = out.rearrange("(n a) j l -> n a j l", a=ROW_TILES)
 
     with ExitStack() as stack:
@@ -109,15 +116,17 @@ def tile_skill_net_pa_t_kernel(tc, s, ei1, ej1, w11, b11, w12, b12, out):
 
         def copy_weights(q, x):
             if x == 0:
-                weight_grouped[q] = grouped.tile([P, 4 * P * 4], BF16, name="w_grouped", align_bytes=64)
+                weight_grouped[q] = grouped.tile(
+                    [P, 2 * 2 * P * PACK], BF16, name="w_grouped", align_bytes=64
+                )
             view = weight_grouped[q][:].bitcast(F32).rearrange(
                 "p (x t m u) -> p x t m u", x=2, t=2, u=2
             )
             side_by_side(nc.scalar.copy, ("w", q, x), view[:, x])
 
         def quantise_weights(q):
-            weight_codes[q] = packed.tile([P, 4 * P], U32, name="w_codes", align_bytes=64)
-            weight_scales[q] = packed.tile([P, 4 * P], U8, name="w_scales", align_bytes=64)
+            weight_codes[q] = packed.tile([P, 2 * 2 * P], U32, name="w_codes", align_bytes=64)
+            weight_scales[q] = packed.tile([P, 2 * 2 * P], U8, name="w_scales", align_bytes=64)
             nc.vector.quantize_mx(
                 out=weight_codes[q][:].bitcast(FP8X4),
                 scales=weight_scales[q][:],
@@ -129,7 +138,7 @@ def tile_skill_net_pa_t_kernel(tc, s, ei1, ej1, w11, b11, w12, b12, out):
 
         def copy_rows(j, half):
             if half == 0:
-                row_grouped[j] = grouped.tile([P, ROWS * 4], BF16, name="s_grouped", align_bytes=64)
+                row_grouped[j] = grouped.tile([P, ROWS * PACK], BF16, name="s_grouped", align_bytes=64)
             view = row_grouped[j][:].bitcast(F32).rearrange("p (a n u) -> p a n u", a=ROW_TILES, u=2)
             side_by_side(nc.vector.tensor_copy, ("s", j, half), view[:, 2 * half : 2 * half + 2])
 
@@ -145,7 +154,7 @@ def tile_skill_net_pa_t_kernel(tc, s, ei1, ej1, w11, b11, w12, b12, out):
         def spread_row_factor(j):
             bank = psum.tile([P, ROW_TILES, P], F32, name="forward", tag="forward")
             for a in range(ROW_TILES):
-                column = TILE_ROWS + a * MODULES + j
+                column = UNIT_COLUMNS + a * MODULES + j
                 nc.tensor.transpose(
                     bank[:, a, :], factor[:, column : column + 1].to_broadcast([P, P]), ident[:]
                 )
@@ -161,11 +170,11 @@ def tile_skill_net_pa_t_kernel(tc, s, ei1, ej1, w11, b11, w12, b12, out):
             j = q // STEPS_PER_MODULE
             for t in range(2):
                 bank = psum.tile([P, ROWS], F32, name=tag, tag=tag)
-                columns = slice((2 * x + t) * P, (2 * x + t + 1) * P)
+                tile_columns = slice((2 * x + t) * P, (2 * x + t + 1) * P)
                 nc.tensor.matmul_mx(
                     out=bank[:],
-                    lhsT=weight_codes[q][:, columns].bitcast(FP8X4),
-                    lhsT_scale=weight_scales[q][:, columns],
+                    lhsT=weight_codes[q][:, tile_columns].bitcast(FP8X4),
+                    lhsT_scale=weight_scales[q][:, tile_columns],
                     rhs=row_codes[j][:].bitcast(FP8X4),
                     rhs_scale=row_scales[j][:],
                     start=True,
@@ -227,11 +236,11 @@ def tile_skill_net_pa_t_kernel(tc, s, ei1, ej1, w11, b11, w12, b12, out):
         def relu_out(q, t, on_vector):
             if t == 0:
                 out_pair[q] = result.tile([P, ROW_TILES, 2 * P], F32, name="out_pair")
-            columns = out_pair[q][:, :, t * P : (t + 1) * P]
+            out_tile = out_pair[q][:, :, t * P : (t + 1) * P]
             if on_vector:
-                nc.vector.tensor_scalar_max(out=columns, in0=backward_bank[(q, t)][:], scalar1=0.0)
+                nc.vector.tensor_scalar_max(out=out_tile, in0=backward_bank[(q, t)][:], scalar1=0.0)
             else:
-                nc.scalar.activation(out=columns, in_=backward_bank[(q, t)][:], func=ACT.Relu)
+                nc.scalar.activation(out=out_tile, in_=backward_bank[(q, t)][:], func=ACT.Relu)
 
         def store(q):
             j, first_unit = q // STEPS_PER_MODULE, 2 * P * (q % STEPS_PER_MODULE)
@@ -242,49 +251,53 @@ def tile_skill_net_pa_t_kernel(tc, s, ei1, ej1, w11, b11, w12, b12, out):
         ident = const.tile([P, P], F32, name="ident")
         make_identity(nc, ident[:])
 
-        rows_bf16 = const.tile([P, 2, P], BF16, name="rows_bf16")
-        nc.vector.memset(rows_bf16[:], 0.0)
-        ei_bf16 = const.tile([P, ROW_DRAWS], BF16, name="ei_bf16")
+        lines_bf16 = const.tile([P, 2, P], BF16, name="lines_bf16")
+        nc.vector.memset(lines_bf16[:], 0.0)
+        ei_bf16 = const.tile([P, ROW_COLUMNS], BF16, name="ei_bf16")
         nc.sync.dma_start(out=ei_bf16[:], in_=ei1.rearrange("(n a) j o -> n (a j o)", a=ROW_TILES))
-        nc.sync.dma_start(out=rows_bf16[0:TILE_ROWS, 1, :], in_=ej1.rearrange("o j (t m) -> (o j t) m", m=P))
-        nc.sync.dma_start(out=rows_bf16[0:TILE_ROWS, 0, :], in_=b11.rearrange("j (t m) -> (j t) m", m=P))
-        nc.sync.dma_start(out=rows_bf16[TILE_ROWS:P, 0, :], in_=b12.rearrange("j (t m) -> (j t) m", m=P))
+        nc.sync.dma_start(
+            out=lines_bf16[0:UNIT_COLUMNS, 1, :], in_=ej1.rearrange("o j (g m) -> (o j g) m", m=P)
+        )
+        nc.sync.dma_start(out=lines_bf16[0:UNIT_COLUMNS, 0, :], in_=b11.rearrange("j (g m) -> (j g) m", m=P))
+        nc.sync.dma_start(out=lines_bf16[UNIT_COLUMNS:P, 0, :], in_=b12.rearrange("j (g m) -> (j g) m", m=P))
         for q in range(LOAD_AHEAD):
             load_for_pair(q)
 
-        rows_f32 = const.tile([P, 2, P], F32, name="rows_f32")
-        nc.vector.tensor_copy(out=rows_f32[:], in_=rows_bf16[:])
-        vector_bank = psum.tile([P, 2, P], F32, name="forward", tag="forward")
-        for plane in range(2):
-            nc.tensor.transpose(vector_bank[:, plane, :], rows_f32[:, plane, :], ident[:])
-        b11_columns = const.tile([P, TILE_ROWS], F32, name="b11_columns")
-        nc.vector.tensor_copy(out=b11_columns[:], in_=vector_bank[:, 0, 0:TILE_ROWS])
-        b12_columns = const.tile([P, TILE_ROWS], F32, name="b12_columns")
-        nc.vector.tensor_copy(out=b12_columns[:], in_=vector_bank[:, 0, TILE_ROWS:P])
+        lines_f32 = const.tile([P, 2, P], F32, name="lines_f32")
+        nc.vector.tensor_copy(out=lines_f32[:], in_=lines_bf16[:])
+        column_bank = psum.tile([P, 2, P], F32, name="forward", tag="forward")
+        for sheet in range(2):
+            nc.tensor.transpose(column_bank[:, sheet, :], lines_f32[:, sheet, :], ident[:])
+        b11_columns = const.tile([P, UNIT_COLUMNS], F32, name="b11_columns")
+        nc.vector.tensor_copy(out=b11_columns[:], in_=column_bank[:, 0, 0:UNIT_COLUMNS])
+        b12_columns = const.tile([P, UNIT_COLUMNS], F32, name="b12_columns")
+        nc.vector.tensor_copy(out=b12_columns[:], in_=column_bank[:, 0, UNIT_COLUMNS:P])
 
-        draws = const.tile([P, TILE_ROWS + ROW_DRAWS], F32, name="draws")
-        nc.vector.tensor_copy(out=draws[:, 0:TILE_ROWS], in_=vector_bank[:, 1, 0:TILE_ROWS])
-        nc.vector.tensor_copy(out=draws[:, TILE_ROWS:], in_=ei_bf16[:])
-        magnitude = const.tile([P, TILE_ROWS + ROW_DRAWS], F32, name="magnitude")
+        draws = const.tile([P, UNIT_COLUMNS + ROW_COLUMNS], F32, name="draws")
+        nc.vector.tensor_copy(out=draws[:, 0:UNIT_COLUMNS], in_=column_bank[:, 1, 0:UNIT_COLUMNS])
+        nc.vector.tensor_copy(out=draws[:, UNIT_COLUMNS:], in_=ei_bf16[:])
+        magnitude = const.tile([P, UNIT_COLUMNS + ROW_COLUMNS], F32, name="magnitude")
         nc.vector.scalar_tensor_tensor(
             out=magnitude[:], in0=draws[:], scalar=-1.0, in1=draws[:], op0=ALU.mult, op1=ALU.max
         )
-        root = const.tile([P, TILE_ROWS + ROW_DRAWS], F32, name="root")
-        nc.scalar.activation(out=root[:], in_=magnitude[:], func=ACT.Sqrt)
-        signs = const.tile([P, TILE_ROWS + ROW_DRAWS], F32, name="signs")
+        lifted = const.tile([P, UNIT_COLUMNS + ROW_COLUMNS], F32, name="lifted")
+        nc.vector.tensor_scalar_max(out=lifted[:], in0=magnitude[:], scalar1=SQRT_MIN)
+        root = const.tile([P, UNIT_COLUMNS + ROW_COLUMNS], F32, name="root")
+        nc.scalar.activation(out=root[:], in_=lifted[:], func=ACT.Sqrt)
+        signs = const.tile([P, UNIT_COLUMNS + ROW_COLUMNS], F32, name="signs")
         nc.scalar.activation(out=signs[:], in_=draws[:], func=ACT.Sign)
-        factor = const.tile([P, TILE_ROWS + ROW_DRAWS], F32, name="factor")
+        factor = const.tile([P, UNIT_COLUMNS + ROW_COLUMNS], F32, name="factor")
         nc.vector.tensor_mul(out=factor[:], in0=signs[:], in1=root[:])
 
-        for q in range(-4, PAIRS + 2):
-            phase = q % STEPS_PER_MODULE
+        for q in range(-TRANSPOSE_AHEAD, PAIRS + RELU_BEHIND):
+            step_in_module = q % STEPS_PER_MODULE
             coming = q // STEPS_PER_MODULE + 1
-            extra_rows = coming < MODULES and phase < 2
-            extra_factor = coming < MODULES and phase == 3
+            extra_rows = coming < MODULES and step_in_module < 2
+            extra_factor = coming < MODULES and step_in_module == 3
             vector_is_done = q >= PAIRS
 
-            if q + 4 + LOAD_AHEAD < PAIRS:
-                load_for_pair(q + 4 + LOAD_AHEAD)
+            if q + TRANSPOSE_AHEAD + LOAD_AHEAD < PAIRS:
+                load_for_pair(q + TRANSPOSE_AHEAD + LOAD_AHEAD)
 
             if 0 <= q < PAIRS:
                 exponentials(q)
@@ -292,41 +305,41 @@ def tile_skill_net_pa_t_kernel(tc, s, ei1, ej1, w11, b11, w12, b12, out):
             if 0 <= q + 1 < PAIRS:
                 multiply(q + 1, 0, log_sigma_bank, "log_sigma")
 
-            if 0 <= q + 3 < PAIRS:
-                copy_weights(q + 3, 0)
+            if 0 <= q + COPY_AHEAD < PAIRS:
+                copy_weights(q + COPY_AHEAD, 0)
             if extra_rows:
-                transpose_rows(coming, phase)
+                transpose_rows(coming, step_in_module)
             if extra_factor:
                 spread_row_factor(coming)
-            if 0 <= q - 2 < PAIRS:
-                relu_out(q - 2, 0, False)
-            if 0 <= q - 1 < PAIRS:
-                transpose_back(q - 1, 0)
-            if 0 <= q + 3 < PAIRS:
-                copy_weights(q + 3, 1)
-            if q + 4 < PAIRS:
-                transpose_weights(q + 4, 0)
+            if 0 <= q - RELU_BEHIND < PAIRS:
+                relu_out(q - RELU_BEHIND, 0, False)
+            if 0 <= q - BACK_BEHIND < PAIRS:
+                transpose_back(q - BACK_BEHIND, 0)
+            if 0 <= q + COPY_AHEAD < PAIRS:
+                copy_weights(q + COPY_AHEAD, 1)
+            if q + TRANSPOSE_AHEAD < PAIRS:
+                transpose_weights(q + TRANSPOSE_AHEAD, 0)
 
             if 0 <= q < PAIRS:
                 multiply(q, 1, mu_bank, "mu")
 
-            if 0 <= q - 2 < PAIRS:
-                relu_out(q - 2, 1, vector_is_done)
-                store(q - 2)
-            if 0 <= q - 1 < PAIRS:
-                transpose_back(q - 1, 1)
+            if 0 <= q - RELU_BEHIND < PAIRS:
+                relu_out(q - RELU_BEHIND, 1, vector_is_done)
+                store(q - RELU_BEHIND)
+            if 0 <= q - BACK_BEHIND < PAIRS:
+                transpose_back(q - BACK_BEHIND, 1)
 
-            if 0 <= q + 2 < PAIRS:
-                quantise_weights(q + 2)
-            if coming < MODULES and phase == 2:
+            if 0 <= q + QUANTISE_AHEAD < PAIRS:
+                quantise_weights(q + QUANTISE_AHEAD)
+            if coming < MODULES and step_in_module == 2:
                 quantise_rows(coming)
             if 0 <= q < PAIRS:
                 scale_noise(q)
             if extra_rows:
-                copy_rows(coming, phase)
+                copy_rows(coming, step_in_module)
             if extra_factor:
                 copy_row_factor(coming)
-            if q + 4 < PAIRS:
-                transpose_weights(q + 4, 1)
+            if q + TRANSPOSE_AHEAD < PAIRS:
+                transpose_weights(q + TRANSPOSE_AHEAD, 1)
             if 0 <= q < PAIRS:
                 add_mu(q)

import math
from contextlib import ExitStack

import concourse.mybir as mybir
from concourse.masks import make_identity

F32 = mybir.dt.float32
BF16 = mybir.dt.bfloat16
U32 = mybir.dt.uint32
U8 = mybir.dt.uint8
FP8X4 = mybir.dt.float8_e4m3fn_x4
ACT = mybir.ActivationFunctionType
ALU = mybir.AluOpType

P = 128
PACK = 4
MODULES = 8
ROWS = 512
FEATURES = 512
UNITS = 1024
ROW_TILES = ROWS // P
UNIT_TILES = UNITS // P
WORDS = FEATURES // 2
STEPS_PER_MODULE = UNIT_TILES // 2
PAIRS = MODULES * STEPS_PER_MODULE

SIGMA_MAX = math.exp(4.0)
SIGMA_MIN = math.exp(-20.0)
SQRT_MIN = 2.0**-116

UNIT_COLUMNS = MODULES * UNIT_TILES
ROW_COLUMNS = ROW_TILES * MODULES

TRANSPOSE_AHEAD = 4
COPY_AHEAD = 3
QUANTISE_AHEAD = 2
BACK_BEHIND = 1
RELU_BEHIND = 2
LOAD_AHEAD = 6

FLOPS = 2 * 2 * MODULES * ROWS * UNITS * FEATURES


def tile_skill_net_pa_t_kernel(tc, s, ei1, ej1, w11, b11, w12, b12, out):
    nc = tc.nc

    s_view = s.rearrange("(n a) j k -> n a j k", a=ROW_TILES)
    w_views = [w.rearrange("j (g m) k -> j m g k", m=P) for w in (w12, w11)]
    out_view = out.rearrange("(n a) j l -> n a j l", a=ROW_TILES)

    with ExitStack() as stack:
        const = stack.enter_context(tc.tile_pool(name="const", bufs=1))
        raw_weights = stack.enter_context(tc.tile_pool(name="raw_weights", bufs=LOAD_AHEAD + 2))
        raw_rows = stack.enter_context(tc.tile_pool(name="raw_rows", bufs=3))
        grouped = stack.enter_context(tc.tile_pool(name="grouped", bufs=3))
        packed = stack.enter_context(tc.tile_pool(name="packed", bufs=4))
        work = stack.enter_context(tc.tile_pool(name="work", bufs=3))
        result = stack.enter_context(tc.tile_pool(name="result", bufs=4))
        psum = stack.enter_context(tc.psum_pool(name="psum", bufs=2))
        stack.enter_context(tc.manual_schedule())

        weight_words = {}
        row_words = {}
        forward_bank = {}
        weight_grouped = {}
        row_grouped = {}
        weight_codes = {}
        weight_scales = {}
        row_codes = {}
        row_scales = {}
        row_factor = {}
        log_sigma_bank = {}
        mu_bank = {}
        sigma = {}
        summed = {}
        backward_bank = {}
        out_pair = {}

        def load_rows(j):
            s_raw = raw_rows.tile([P, ROW_TILES * FEATURES], BF16, name="s_raw")
            nc.sync.dma_start(
                out=s_raw[:].rearrange("p (a k) -> p a k", a=ROW_TILES), in_=s_view[:, :, j, :]
            )
            row_words[j] = s_raw[:].bitcast(F32)

        def load_weights(q):
            j, first_tile = q // STEPS_PER_MODULE, 2 * (q % STEPS_PER_MODULE)
            w_raw = raw_weights.tile([P, 2 * 2 * FEATURES], BF16, name="w_raw")
            for x in range(2):
                nc.sync.dma_start(
                    out=w_raw[:, x * 2 * FEATURES : (x + 1) * 2 * FEATURES].rearrange(
                        "p (t k) -> p t k", t=2
                    ),
                    in_=w_views[x][j, :, first_tile : first_tile + 2, :],
                )
            weight_words[q] = w_raw[:].bitcast(F32)

        def load_for_pair(q):
            if q % STEPS_PER_MODULE == 0:
                load_rows(q // STEPS_PER_MODULE)
            load_weights(q)

        def transpose_two_tiles(words, first_word, key):
            bank = psum.tile([P, 2, 2, P], F32, name="forward", tag="forward")
            for t in range(2):
                for u in range(2):
                    start = first_word + t * WORDS + u * P
                    nc.tensor.transpose(bank[:, t, u, :], words[:, start : start + P], ident[:])
            forward_bank[key] = bank

        def side_by_side(copy, key, grouped_words):
            copy(out=grouped_words, in_=forward_bank[key][:].rearrange("p t u r -> p t r u"))

        def transpose_weights(q, x):
            transpose_two_tiles(weight_words[q], x * 2 * WORDS, ("w", q, x))

        def copy_weights(q, x):
            if x == 0:
                weight_grouped[q] = grouped.tile(
                    [P, 2 * 2 * P * PACK], BF16, name="w_grouped", align_bytes=64
                )
            view = weight_grouped[q][:].bitcast(F32).rearrange(
                "p (x t m u) -> p x t m u", x=2, t=2, u=2
            )
            side_by_side(nc.scalar.copy, ("w", q, x), view[:, x])

        def quantise_weights(q):
            weight_codes[q] = packed.tile([P, 2 * 2 * P], U32, name="w_codes", align_bytes=64)
            weight_scales[q] = packed.tile([P, 2 * 2 * P], U8, name="w_scales", align_bytes=64)
            nc.vector.quantize_mx(
                out=weight_codes[q][:].bitcast(FP8X4),
                scales=weight_scales[q][:],
                in_=weight_grouped[q][:],
            )

        def transpose_rows(j, half):
            transpose_two_tiles(row_words[j], half * 2 * WORDS, ("s", j, half))

        def copy_rows(j, half):
            if half == 0:
                row_grouped[j] = grouped.tile([P, ROWS * PACK], BF16, name="s_grouped", align_bytes=64)
            view = row_grouped[j][:].bitcast(F32).rearrange("p (a n u) -> p a n u", a=ROW_TILES, u=2)
            side_by_side(nc.vector.tensor_copy, ("s", j, half), view[:, 2 * half : 2 * half + 2])

        def quantise_rows(j):
            row_codes[j] = packed.tile([P, ROWS], U32, name="s_codes", align_bytes=64)
            row_scales[j] = packed.tile([P, ROWS], U8, name="s_scales", align_bytes=64)
            nc.vector.quantize_mx(
                out=row_codes[j][:].bitcast(FP8X4),
                scales=row_scales[j][:],
                in_=row_grouped[j][:],
            )

        def spread_row_factor(j):
            bank = psum.tile([P, ROW_TILES, P], F32, name="forward", tag="forward")
            for a in range(ROW_TILES):
                column = UNIT_COLUMNS + a * MODULES + j
                nc.tensor.transpose(
                    bank[:, a, :], factor[:, column : column + 1].to_broadcast([P, P]), ident[:]
                )
            forward_bank[("f", j)] = bank

        def copy_row_factor(j):
            row_factor[j] = work.tile([P, ROWS], F32, name="row_factor")
            nc.vector.tensor_copy(
                out=row_factor[j][:], in_=forward_bank[("f", j)][:].rearrange("p a n -> p (a n)")
            )

        def multiply(q, x, banks, tag):
            j = q // STEPS_PER_MODULE
            for t in range(2):
                bank = psum.tile([P, ROWS], F32, name=tag, tag=tag)
                tile_columns = slice((2 * x + t) * P, (2 * x + t + 1) * P)
                nc.tensor.matmul_mx(
                    out=bank[:],
                    lhsT=weight_codes[q][:, tile_columns].bitcast(FP8X4),
                    lhsT_scale=weight_scales[q][:, tile_columns],
                    rhs=row_codes[j][:].bitcast(FP8X4),
                    rhs_scale=row_scales[j][:],
                    start=True,
                    stop=True,
                )
                banks[(q, t)] = bank

        def exponentials(q):
            sigma[q] = work.tile([P, 2, ROWS], F32, name="sigma")
            for t in range(2):
                nc.scalar.activation(
                    out=sigma[q][:, t, :],
                    in_=log_sigma_bank[(q, t)][:],
                    func=ACT.Exp,
                    bias=b12_columns[:, 2 * q + t : 2 * q + t + 1],
                    scale=1.0,
                )

        def clip_sigma(q):
            for t in range(2):
                nc.gpsimd.tensor_scalar(
                    out=sigma[q][:, t, :],
                    in0=sigma[q][:, t, :],
                    scalar1=SIGMA_MAX,
                    scalar2=SIGMA_MIN,
                    op0=ALU.min,
                    op1=ALU.max,
                )

        def scale_noise(q):
            for t in range(2):
                nc.vector.scalar_tensor_tensor(
                    out=sigma[q][:, t, :],
                    in0=sigma[q][:, t, :],
                    scalar=factor[:, 2 * q + t : 2 * q + t + 1],
                    in1=row_factor[q // STEPS_PER_MODULE][:],
                    op0=ALU.mult,
                    op1=ALU.mult,
                )

        def add_mu(q):
            summed[q] = work.tile([P, 2, ROWS], F32, name="summed")
            for t in range(2):
                nc.vector.scalar_tensor_tensor(
                    out=summed[q][:, t, :],
                    in0=mu_bank[(q, t)][:],
                    scalar=b11_columns[:, 2 * q + t : 2 * q + t + 1],
                    in1=sigma[q][:, t, :],
                    op0=ALU.add,
                    op1=ALU.add,
                )

        def transpose_back(q, t):
            bank = psum.tile([P, ROW_TILES, P], F32, name="backward", tag="backward")
            for a in range(ROW_TILES):
                nc.tensor.transpose(bank[:, a, :], summed[q][:, t, a * P : (a + 1) * P], ident[:])
            backward_bank[(q, t)] = bank

        def relu_out(q, t, on_vector):
            if t == 0:
                out_pair[q] = result.tile([P, ROW_TILES, 2 * P], F32, name="out_pair")
            out_tile = out_pair[q][:, :, t * P : (t + 1) * P]
            if on_vector:
                nc.vector.tensor_scalar_max(out=out_tile, in0=backward_bank[(q, t)][:], scalar1=0.0)
            else:
                nc.scalar.activation(out=out_tile, in_=backward_bank[(q, t)][:], func=ACT.Relu)

        def store(q):
            j, first_unit = q // STEPS_PER_MODULE, 2 * P * (q % STEPS_PER_MODULE)
            nc.sync.dma_start(
                out=out_view[:, :, j, first_unit : first_unit + 2 * P], in_=out_pair[q][:]
            )

        ident = const.tile([P, P], F32, name="ident")
        make_identity(nc, ident[:])

        lines_bf16 = const.tile([P, 2, P], BF16, name="lines_bf16")
        nc.vector.memset(lines_bf16[:], 0.0)
        ei_bf16 = const.tile([P, ROW_COLUMNS], BF16, name="ei_bf16")
        nc.sync.dma_start(out=ei_bf16[:], in_=ei1.rearrange("(n a) j o -> n (a j o)", a=ROW_TILES))
        nc.sync.dma_start(
            out=lines_bf16[0:UNIT_COLUMNS, 1, :], in_=ej1.rearrange("o j (g m) -> (o j g) m", m=P)
        )
        nc.sync.dma_start(out=lines_bf16[0:UNIT_COLUMNS, 0, :], in_=b11.rearrange("j (g m) -> (j g) m", m=P))
        nc.sync.dma_start(out=lines_bf16[UNIT_COLUMNS:P, 0, :], in_=b12.rearrange("j (g m) -> (j g) m", m=P))
        for q in range(LOAD_AHEAD):
            load_for_pair(q)

        lines_f32 = const.tile([P, 2, P], F32, name="lines_f32")
        nc.vector.tensor_copy(out=lines_f32[:], in_=lines_bf16[:])
        column_bank = psum.tile([P, 2, P], F32, name="forward", tag="forward")
        for sheet in range(2):
            nc.tensor.transpose(column_bank[:, sheet, :], lines_f32[:, sheet, :], ident[:])
        b11_columns = const.tile([P, UNIT_COLUMNS], F32, name="b11_columns")
        nc.vector.tensor_copy(out=b11_columns[:], in_=column_bank[:, 0, 0:UNIT_COLUMNS])
        b12_columns = const.tile([P, UNIT_COLUMNS], F32, name="b12_columns")
        nc.vector.tensor_copy(out=b12_columns[:], in_=column_bank[:, 0, UNIT_COLUMNS:P])

        draws = const.tile([P, UNIT_COLUMNS + ROW_COLUMNS], F32, name="draws")
        nc.vector.tensor_copy(out=draws[:, 0:UNIT_COLUMNS], in_=column_bank[:, 1, 0:UNIT_COLUMNS])
        nc.vector.tensor_copy(out=draws[:, UNIT_COLUMNS:], in_=ei_bf16[:])
        magnitude = const.tile([P, UNIT_COLUMNS + ROW_COLUMNS], F32, name="magnitude")
        nc.vector.scalar_tensor_tensor(
            out=magnitude[:], in0=draws[:], scalar=-1.0, in1=draws[:], op0=ALU.mult, op1=ALU.max
        )
        lifted = const.tile([P, UNIT_COLUMNS + ROW_COLUMNS], F32, name="lifted")
        nc.vector.tensor_scalar_max(out=lifted[:], in0=magnitude[:], scalar1=SQRT_MIN)
        root = const.tile([P, UNIT_COLUMNS + ROW_COLUMNS], F32, name="root")
        nc.scalar.activation(out=root[:], in_=lifted[:], func=ACT.Sqrt)
        signs = const.tile([P, UNIT_COLUMNS + ROW_COLUMNS], F32, name="signs")
        nc.scalar.activation(out=signs[:], in_=draws[:], func=ACT.Sign)
        factor = const.tile([P, UNIT_COLUMNS + ROW_COLUMNS], F32, name="factor")
        nc.vector.tensor_mul(out=factor[:], in0=signs[:], in1=root[:])

        for q in range(-TRANSPOSE_AHEAD, PAIRS + RELU_BEHIND):
            step_in_module = q % STEPS_PER_MODULE
            coming = q // STEPS_PER_MODULE + 1
            extra_rows = coming < MODULES and step_in_module < 2
            extra_factor = coming < MODULES and step_in_module == 3
            vector_is_done = q >= PAIRS

            if q + TRANSPOSE_AHEAD + LOAD_AHEAD < PAIRS:
                load_for_pair(q + TRANSPOSE_AHEAD + LOAD_AHEAD)

            if 0 <= q < PAIRS:
                exponentials(q)
                clip_sigma(q)
            if 0 <= q + 1 < PAIRS:
                multiply(q + 1, 0, log_sigma_bank, "log_sigma")

            if 0 <= q + COPY_AHEAD < PAIRS:
                copy_weights(q + COPY_AHEAD, 0)
            if extra_rows:
                transpose_rows(coming, step_in_module)
            if extra_factor:
                spread_row_factor(coming)
            if 0 <= q - RELU_BEHIND < PAIRS:
                relu_out(q - RELU_BEHIND, 0, False)
            if 0 <= q - BACK_BEHIND < PAIRS:
                transpose_back(q - BACK_BEHIND, 0)
            if 0 <= q + COPY_AHEAD < PAIRS:
                copy_weights(q + COPY_AHEAD, 1)
            if q + TRANSPOSE_AHEAD < PAIRS:
                transpose_weights(q + TRANSPOSE_AHEAD, 0)

            if 0 <= q < PAIRS:
                multiply(q, 1, mu_bank, "mu")

            if 0 <= q - RELU_BEHIND < PAIRS:
                relu_out(q - RELU_BEHIND, 1, vector_is_done)
                store(q - RELU_BEHIND)
            if 0 <= q - BACK_BEHIND < PAIRS:
                transpose_back(q - BACK_BEHIND, 1)

            if 0 <= q + QUANTISE_AHEAD < PAIRS:
                quantise_weights(q + QUANTISE_AHEAD)
            if coming < MODULES and step_in_module == 2:
                quantise_rows(coming)
            if 0 <= q < PAIRS:
                scale_noise(q)
            if extra_rows:
                copy_rows(coming, step_in_module)
            if extra_factor:
                copy_row_factor(coming)
            if q + TRANSPOSE_AHEAD < PAIRS:
                transpose_weights(q + TRANSPOSE_AHEAD, 1)
            if 0 <= q < PAIRS:
                add_mu(q)
